import numpy as np
import ml_dtypes


def mxq(x, axis, fmt="e4m3"):
    dtype, down = {"e4m3": (ml_dtypes.float8_e4m3fn, 7), "e5m2": (ml_dtypes.float8_e5m2, 14)}[fmt]
    v = np.moveaxis(np.asarray(x, np.float32).astype(ml_dtypes.bfloat16).astype(np.float64), axis, -1)
    blocks = v.reshape(v.shape[:-1] + (-1, 32))
    amax = np.abs(blocks).max(-1, keepdims=True)
    byte = np.maximum(np.where(amax > 0, np.frexp(amax)[1] - 1 + 127, 0) - down, 1)
    scale = np.exp2(byte - 127.0)
    codes = (blocks / scale).astype(np.float32).astype(dtype).astype(np.float64)
    return np.moveaxis((codes * scale).reshape(v.shape), -1, axis)


WIDE = False


def mx_kscale(k):
    if not WIDE:
        return np.ones(k)
    levels = np.array([10, -10, 5, -5, 0])
    if k % 512:
        return np.exp2(np.random.permutation(np.resize(levels, k // 32))).repeat(32)
    a = np.empty((k // 512, 16))
    for p in range(k // 512):
        a[p, :8] = np.random.permutation(np.resize(levels, 8))
        for g in range(8):
            far = levels[np.abs(levels - a[p, g]) >= 10]
            a[p, g + 8] = far[np.random.randint(len(far))]
    return np.exp2(a.ravel()).repeat(32)


BF16 = ml_dtypes.bfloat16


def bf(x):
    return np.asarray(x, np.float32).astype(BF16)


def f64(x):
    return np.asarray(x).astype(np.float64)


T, B, D, U, V, E = 2, 512, 512, 256, 512, 8
G = 2 * E
K = V * E


def softmax(v):
    e = np.exp(v - v.max(-1, keepdims=True))
    return e / e.sum(-1, keepdims=True)


def setup_inputs():
    rn = np.random.standard_normal
    s = mx_kscale(B)
    sv = mx_kscale(K)[::E]
    th0 = bf(np.abs(rn((T, B, U))) * 0.55)
    share_h = bf(np.abs(rn((B, U))) * 0.5)
    ews1 = bf(rn((U, V, E)) * 2.0 / np.sqrt(U))
    ebs1 = bf(rn((V, E)) * 0.5)
    ew0 = bf(rn((T, U, V, E)) * 2.0 / np.sqrt(U))
    eb1 = bf(rn((T, V, E)) * 0.5)
    gate_pre1 = bf(rn((T, B, G)))
    gb1 = bf(rn((T, G)) * 0.5)
    g = bf(rn((T, B, V)) * np.exp2(np.random.randint(-6, 1, (T, B, 1))) * 8.0 / s[None, :, None] * sv[None, None, :])
    zt = (f64(th0) @ f64(ew0).reshape(T, U, K)).reshape(T, B, V, E) + f64(eb1)[:, None]
    gate = softmax(f64(gate_pre1) + f64(gb1)[:, None])
    return {
        "task_h": bf(f64(th0) * s[None, :, None]),
        "share_h": share_h,
        "ews1": ews1,
        "ebs1": ebs1,
        "ew1": bf(f64(ew0) / sv[None, None, :, None]),
        "eb1": eb1,
        "gate_pre1": gate_pre1,
        "gb1": gb1,
        "zt": np.asarray(zt, np.float32),
        "gate": np.asarray(gate, np.float32),
        "grad_out": g,
    }


def reference(task_h, share_h, ews1, ebs1, ew1, eb1, gate_pre1, gb1, zt, gate, grad_out):
    dz = f64(grad_out)[:, :, :, None] * f64(gate)[:, :, None, :E] * (f64(zt) > 0.0)
    dz = dz.reshape(T, B, K)
    w = f64(ew1).reshape(T, U, K)
    dx = mxq(dz, 2, "e5m2") @ mxq(w, 2, "e4m3").transpose(0, 2, 1)
    dw = mxq(f64(task_h), 1, "e4m3").transpose(0, 2, 1) @ mxq(dz, 1, "e5m2")
    return dx, dw.reshape(T, U, V, E)

@@ -1,0 +1,240 @@
+from contextlib import ExitStack
+
+import concourse.mybir as mybir
+from concourse.masks import make_identity
+
+T, B, U, V, E = 2, 512, 256, 512, 8
+G16 = 16
+K = V * E
+FLOPS = 2 * (2 * T * B * K * U)
+BYTES = T * B * U * 2 + T * U * K * 2 + T * B * K * 4 + T * B * G16 * 4 + T * B * V * 2 + T * B * U * 4 + T * U * K * 4
+
+F32 = mybir.dt.float32
+BF16 = mybir.dt.bfloat16
+U32 = mybir.dt.uint32
+U8 = mybir.dt.uint8
+E4 = mybir.dt.float8_e4m3fn_x4
+E5 = mybir.dt.float8_e5m2_x4
+ALU = mybir.AluOpType
+
+P = 128
+J = 4
+KP = 512
+NG = K // KP
+VC = KP // E
+UB = U // P
+
+
+def tile_plelayer_pb_v_kernel(
+    tc, task_h, share_h, ews1, ebs1, ew1, eb1, gate_pre1, gb1, zt, gate, grad_out, out_0, out_1
+):
+    nc = tc.nc
+    chunks = [(t, g) for t in range(T) for g in range(NG)]
+    n = len(chunks)
+
+    with ExitStack() as ctx:
+        const = ctx.enter_context(tc.tile_pool(name="const", bufs=1))
+        ztp = ctx.enter_context(tc.tile_pool(name="ztp", bufs=6))
+        work = ctx.enter_context(tc.tile_pool(name="work", bufs=3))
+        two = ctx.enter_context(tc.tile_pool(name="two", bufs=2))
+        accp = ctx.enter_context(tc.psum_pool(name="accp", bufs=1))
+        tpp = ctx.enter_context(tc.psum_pool(name="tpp", bufs=3))
+        dwp = ctx.enter_context(tc.psum_pool(name="dwp", bufs=3))
+
+        ident = const.tile([P, P], F32, name="ident")
+        make_identity(nc, ident[:])
+
+        gate_sb = const.tile([P, T, J, G16], F32, name="gate_sb")
+        nc.sync.dma_start(out=gate_sb[:], in_=gate.rearrange("t (p j) g -> p t j g", j=J))
+        g_sb = const.tile([P, T, J, V], BF16, name="g_sb")
+        h_sb = const.tile([P, T, J, U], BF16, name="h_sb")
+        w_sb = const.tile([P, T, UB, K], BF16, name="w_sb")
+        nc.sync.dma_start(out=g_sb[:, 0], in_=grad_out[0].rearrange("(p j) v -> p j v", j=J))
+
+        zt_tiles = {}
+
+        def load_zt(i):
+            t, g = chunks[i]
+            z = ztp.tile([P, J, KP], F32, name="z")
+            src = zt[t].rearrange("(p j) v e -> p j (v e)", j=J)
+            nc.sync.dma_start(out=z[:], in_=src[:, :, g * KP : (g + 1) * KP])
+            zt_tiles[i] = z
+
+        def load_w(t, ub):
+            src = ew1[t].rearrange("(ub p) v e -> p ub (v e)", p=P)
+            nc.sync.dma_start(out=w_sb[:, t, ub, :], in_=src[:, ub, :])
+
+        load_zt(0)
+        nc.sync.dma_start(out=h_sb[:], in_=task_h.rearrange("t (p j) u -> p t j u", j=J))
+        load_w(0, 0)
+        load_zt(1)
+        load_w(0, 1)
+        load_zt(2)
+        nc.sync.dma_start(out=g_sb[:, 1], in_=grad_out[1].rearrange("(p j) v -> p j v", j=J))
+        load_zt(3)
+        load_w(1, 0)
+        load_zt(4)
+        load_w(1, 1)
+        load_zt(5)
+
+        h_codes = const.tile([P, T, U], U32, name="h_codes", align_bytes=64)
+        h_scales = const.tile([P, T, U], U8, name="h_scales", align_bytes=64)
+        for t in range(T):
+            h_grp = two.tile([P, U, J], BF16, name="h_grp", align_bytes=64)
+            nc.scalar.copy(out=h_grp[:], in_=h_sb[:, t].rearrange("p j u -> p u j"))
+            nc.vector.quantize_mx(
+                out=h_codes[:, t, :].bitcast(E4),
+                scales=h_scales[:, t, :],
+                in_=h_grp[:].rearrange("p u j -> p (u j)"),
+            )
+
+        w_codes = const.tile([P, T, NG, U], U32, name="w_codes", align_bytes=64)
+        w_scales = const.tile([P, T, NG, U], U8, name="w_scales", align_bytes=64)
+        w_grps = {}
+
+        def w_transpose(i):
+            t, g = chunks[i]
+            words = w_sb[:, t].rearrange("p ub k -> p (ub k)").bitcast(F32)
+            wt = tpp.tile([P, UB, 2, P], F32, name="tp")
+            for ub in range(UB):
+                for u in range(2):
+                    lo = ub * (K // 2) + g * (KP // 2)
+                    nc.tensor.transpose(wt[:, ub, u, :], words[:, lo + u : lo + KP // 2 : 2], ident[:])
+            w_grp = work.tile([P, U * J], BF16, name="w_grp", align_bytes=64)
+            nc.scalar.copy(
+                out=w_grp[:].bitcast(F32).rearrange("p (ub r u) -> p ub r u", ub=UB, u=2),
+                in_=wt[:].rearrange("p ub u r -> p ub r u"),
+            )
+            w_grps[i] = w_grp
+
+        def w_quant(i):
+            t, g = chunks[i]
+            nc.vector.quantize_mx(
+                out=w_codes[:, t, g, :].bitcast(E4), scales=w_scales[:, t, g, :], in_=w_grps.pop(i)[:]
+            )
+
+        dz_tiles = {}
+        dzi_tiles = {}
+        dzt_tiles = {}
+        q_tiles = {}
+        acc = {}
+
+        def make_dz(i):
+            t, g = chunks[i]
+            gg = two.tile([P, J, VC, E], F32, name="gg")
+            nc.vector.tensor_tensor(
+                out=gg[:],
+                in0=g_sb[:, t, :, g * VC : (g + 1) * VC].unsqueeze(3).to_broadcast([P, J, VC, E]),
+                in1=gate_sb[:, t, :, 0:E].unsqueeze(2).to_broadcast([P, J, VC, E]),
+                op=ALU.mult,
+            )
+            dz = work.tile([P, J, KP], BF16, name="dz")
+            nc.vector.scalar_tensor_tensor(
+                out=dz[:].rearrange("p j k -> p (j k)"),
+                in0=zt_tiles.pop(i)[:].rearrange("p j k -> p (j k)"),
+                scalar=0.0,
+                in1=gg[:].rearrange("p j v e -> p (j v e)"),
+                op0=ALU.is_gt,
+                op1=ALU.mult,
+            )
+            dz_tiles[i] = dz
+
+        def relayout(i):
+            dz = dz_tiles.pop(i)
+            dzi = work.tile([P, KP, J], BF16, name="dzi", align_bytes=64)
+            nc.scalar.copy(out=dzi[:], in_=dz[:].rearrange("p j k -> p k j"))
+            dzi_tiles[i] = dzi
+            words = dz[:].rearrange("p j k -> p (j k)").bitcast(F32)
+            dzt = work.tile([P, B * J], BF16, name="dzt", align_bytes=64)
+            dzt_w = dzt[:].bitcast(F32)
+            for hb in range(2):
+                xt = tpp.tile([P, 2, 2, P], F32, name="tp")
+                for jj in range(2):
+                    j = 2 * hb + jj
+                    for u in range(2):
+                        lo = j * (KP // 2)
+                        nc.tensor.transpose(xt[:, jj, u, :], words[:, lo + u : lo + KP // 2 : 2], ident[:])
+                nc.scalar.copy(
+                    out=dzt_w[:, hb * 512 : (hb + 1) * 512].rearrange("p (j r u) -> p j r u", j=2, u=2),
+                    in_=xt[:].rearrange("p j u r -> p j r u"),
+                )
+            dzt_tiles[i] = dzt
+
+        def quant(i):
+            ci = work.tile([P, KP], U32, name="ci", align_bytes=64)
+            si = work.tile([P, KP], U8, name="si", align_bytes=64)
+            nc.vector.quantize_mx(
+                out=ci[:].bitcast(E5), scales=si[:], in_=dzi_tiles.pop(i)[:].rearrange("p k j -> p (k j)")
+            )
+            ct = work.tile([P, B], U32, name="ct", align_bytes=64)
+            stl = work.tile([P, B], U8, name="stl", align_bytes=64)
+            nc.vector.quantize_mx(out=ct[:].bitcast(E5), scales=stl[:], in_=dzt_tiles.pop(i)[:])
+            q_tiles[i] = (ci, si, ct, stl)
+
+        def multiply(i):
+            t, g = chunks[i]
+            ci, si, ct, stl = q_tiles.pop(i)
+            dw_sb = work.tile([P, UB, KP], F32, name="dw_sb")
+            for ub in range(UB):
+                cols = slice(ub * P, (ub + 1) * P)
+                ps = dwp.tile([P, KP], F32, name="dwps")
+                nc.tensor.matmul_mx(
+                    out=ps[:],
+                    lhsT=h_codes[:, t, cols].bitcast(E4),
+                    lhsT_scale=h_scales[:, t, cols],
+                    rhs=ci[:].bitcast(E5),
+                    rhs_scale=si[:],
+                    start=True,
+                    stop=True,
+                )
+                nc.scalar.copy(out=dw_sb[:, ub, :], in_=ps[:])
+            dst = out_1[t].rearrange("(ub p) v e -> p ub (v e)", p=P)
+            nc.sync.dma_start(out=dst[:, :, g * KP : (g + 1) * KP], in_=dw_sb[:])
+            for ub in range(UB):
+                cols = slice(ub * P, (ub + 1) * P)
+                if g == 0:
+                    acc[ub] = accp.tile([P, B], F32, name="acc%d" % ub)
+                nc.tensor.matmul_mx(
+                    out=acc[ub][:],
+                    lhsT=w_codes[:, t, g, cols].bitcast(E4),
+                    lhsT_scale=w_scales[:, t, g, cols],
+                    rhs=ct[:].bitcast(E5),
+                    rhs_scale=stl[:],
+                    start=(g == 0),
+                    stop=(g == NG - 1),
+                )
+            if g == NG - 1:
+                finish_dx(t)
+
+        def finish_dx(t):
+            dxt = two.tile([P, UB, B], F32, name="dxt")
+            for ub in range(UB):
+                nc.scalar.copy(out=dxt[:, ub, :], in_=acc[ub][:])
+            dx_sb = two.tile([P, J, U], F32, name="dx_sb")
+            for hb in range(2):
+                xt = tpp.tile([P, 2, UB, P], F32, name="tp")
+                for jj in range(2):
+                    j = 2 * hb + jj
+                    for ub in range(UB):
+                        nc.tensor.transpose(xt[:, jj, ub, :], dxt[:, ub, j * P : (j + 1) * P], ident[:])
+                nc.scalar.copy(
+                    out=dx_sb[:, 2 * hb : 2 * hb + 2, :].rearrange("p j u -> p (j u)"),
+                    in_=xt[:].rearrange("p j ub r -> p (j ub r)"),
+                )
+            nc.sync.dma_start(out=out_0[t].rearrange("(p j) u -> p j u", j=J), in_=dx_sb[:])
+
+        w_transpose(0)
+        for i in range(n + 1):
+            if i < n:
+                make_dz(i)
+                if i + 6 < n:
+                    load_zt(i + 6)
+                relayout(i)
+                if i + 1 < n:
+                    w_transpose(i + 1)
+            if i >= 1:
+                quant(i - 1)
+            if i < n:
+                w_quant(i)
+            if i >= 1:
+                multiply(i - 1)

@@ -23,6 +23,8 @@ KP = 512
 NG = K // KP
 VC = KP // E
 UB = U // P
+ZB = 6
+GJ = 1
 
 
 def tile_plelayer_pb_v_kernel(
@@ -31,25 +33,35 @@ def tile_plelayer_pb_v_kernel(
     nc = tc.nc
     chunks = [(t, g) for t in range(T) for g in range(NG)]
     n = len(chunks)
+    last = n - 1
 
     with ExitStack() as ctx:
         const = ctx.enter_context(tc.tile_pool(name="const", bufs=1))
-        ztp = ctx.enter_context(tc.tile_pool(name="ztp", bufs=6))
+        ztp = ctx.enter_context(tc.tile_pool(name="ztp", bufs=ZB))
         work = ctx.enter_context(tc.tile_pool(name="work", bufs=3))
         two = ctx.enter_context(tc.tile_pool(name="two", bufs=2))
+        one = ctx.enter_context(tc.tile_pool(name="one", bufs=1))
+        gatep = ctx.enter_context(tc.psum_pool(name="gatep", bufs=1))
         accp = ctx.enter_context(tc.psum_pool(name="accp", bufs=1))
         tpp = ctx.enter_context(tc.psum_pool(name="tpp", bufs=3))
-        dwp = ctx.enter_context(tc.psum_pool(name="dwp", bufs=3))
+        dwp = ctx.enter_context(tc.psum_pool(name="dwp", bufs=2))
+        ctx.enter_context(tc.manual_schedule())
 
         ident = const.tile([P, P], F32, name="ident")
         make_identity(nc, ident[:])
+
+        def copy_on(eng, out, in_):
+            if eng == "v":
+                nc.vector.tensor_copy(out=out, in_=in_)
+            else:
+                nc.scalar.copy(out=out, in_=in_)
 
         gate_sb = const.tile([P, T, J, G16], F32, name="gate_sb")
         nc.sync.dma_start(out=gate_sb[:], in_=gate.rearrange("t (p j) g -> p t j g", j=J))
         g_sb = const.tile([P, T, J, V], BF16, name="g_sb")
         h_sb = const.tile([P, T, J, U], BF16, name="h_sb")
-        w_sb = const.tile([P, T, UB, K], BF16, name="w_sb")
-        nc.sync.dma_start(out=g_sb[:, 0], in_=grad_out[0].rearrange("(p j) v -> p j v", j=J))
+        g_src = grad_out.rearrange("t (p j) v -> p t j v", j=J)
+        nc.sync.dma_start(out=g_sb[:, 0, :, 0 : 2 * VC], in_=g_src[:, 0, :, 0 : 2 * VC])
 
         zt_tiles = {}
 
@@ -60,45 +72,47 @@ def tile_plelayer_pb_v_kernel(
             nc.sync.dma_start(out=z[:], in_=src[:, :, g * KP : (g + 1) * KP])
             zt_tiles[i] = z
 
-        def load_w(t, ub):
+        w_tiles = {}
+
+        def load_w(q):
+            t, pr = q // (NG // 2), q % (NG // 2)
+            w_pair = const.tile([P, UB, 2 * KP], BF16, name="w_pair%d" % q)
             src = ew1[t].rearrange("(ub p) v e -> p ub (v e)", p=P)
-            nc.sync.dma_start(out=w_sb[:, t, ub, :], in_=src[:, ub, :])
+            nc.sync.dma_start(out=w_pair[:], in_=src[:, :, pr * 2 * KP : (pr + 1) * 2 * KP])
+            w_tiles[q] = w_pair
 
         load_zt(0)
-        nc.sync.dma_start(out=h_sb[:], in_=task_h.rearrange("t (p j) u -> p t j u", j=J))
-        load_w(0, 0)
+        nc.sync.dma_start(out=g_sb[:, 0, :, 2 * VC : V], in_=g_src[:, 0, :, 2 * VC : V])
         load_zt(1)
-        load_w(0, 1)
+        load_w(0)
+        nc.sync.dma_start(out=h_sb[:], in_=task_h.rearrange("t (p j) u -> p t j u", j=J))
         load_zt(2)
-        nc.sync.dma_start(out=g_sb[:, 1], in_=grad_out[1].rearrange("(p j) v -> p j v", j=J))
         load_zt(3)
-        load_w(1, 0)
+        load_w(1)
         load_zt(4)
-        load_w(1, 1)
         load_zt(5)
+        nc.sync.dma_start(out=g_sb[:, 1], in_=g_src[:, 1])
+
+        gt_ps = tpp.tile([P, P], F32, name="tp")
+        nc.tensor.transpose(gt_ps[:], gate_sb[:].rearrange("p t j g -> p (t j g)"), ident[:])
+        gate_t = const.tile([P, P], F32, name="gate_t")
+        nc.scalar.copy(out=gate_t[:], in_=gt_ps[:])
+        gate_ps = gatep.tile([P, T, J, G16], F32, name="gate_ps")
+        nc.tensor.transpose(gate_ps[:].rearrange("p t j g -> p (t j g)"), gate_t[:], ident[:])
 
         h_codes = const.tile([P, T, U], U32, name="h_codes", align_bytes=64)
         h_scales = const.tile([P, T, U], U8, name="h_scales", align_bytes=64)
-        for t in range(T):
-            h_grp = two.tile([P, U, J], BF16, name="h_grp", align_bytes=64)
-            nc.scalar.copy(out=h_grp[:], in_=h_sb[:, t].rearrange("p j u -> p u j"))
-            nc.vector.quantize_mx(
-                out=h_codes[:, t, :].bitcast(E4),
-                scales=h_scales[:, t, :],
-                in_=h_grp[:].rearrange("p u j -> p (u j)"),
-            )
-
+        h_grps = []
         w_codes = const.tile([P, T, NG, U], U32, name="w_codes", align_bytes=64)
         w_scales = const.tile([P, T, NG, U], U8, name="w_scales", align_bytes=64)
         w_grps = {}
 
         def w_transpose(i):
-            t, g = chunks[i]
-            words = w_sb[:, t].rearrange("p ub k -> p (ub k)").bitcast(F32)
+            words = w_tiles[i // 2][:].rearrange("p ub k -> p (ub k)").bitcast(F32)
             wt = tpp.tile([P, UB, 2, P], F32, name="tp")
             for ub in range(UB):
                 for u in range(2):
-                    lo = ub * (K // 2) + g * (KP // 2)
+                    lo = ub * KP + (i % 2) * (KP // 2)
                     nc.tensor.transpose(wt[:, ub, u, :], words[:, lo + u : lo + KP // 2 : 2], ident[:])
             w_grp = work.tile([P, U * J], BF16, name="w_grp", align_bytes=64)
             nc.scalar.copy(
@@ -116,18 +130,35 @@ def tile_plelayer_pb_v_kernel(
         dz_tiles = {}
         dzi_tiles = {}
         dzt_tiles = {}
-        q_tiles = {}
+        qi_tiles = {}
+        qt_tiles = {}
         acc = {}
+        pending = []
 
-        def make_dz(i):
+        gg_tiles = {}
+
+        def make_gg(i):
             t, g = chunks[i]
-            gg = two.tile([P, J, VC, E], F32, name="gg")
+            gg = one.tile([P, J, VC, E], F32, name="gg")
+            jv = J - GJ
+            gates = gate_sb if i == 0 else gate_ps
+            if GJ > 0:
+                nc.gpsimd.tensor_tensor(
+                    out=gg[:, jv:J],
+                    in0=g_sb[:, t, jv:J, g * VC : (g + 1) * VC].unsqueeze(3).to_broadcast([P, GJ, VC, E]),
+                    in1=gate_sb[:, t, jv:J, 0:E].unsqueeze(2).to_broadcast([P, GJ, VC, E]),
+                    op=ALU.mult,
+                )
             nc.vector.tensor_tensor(
-                out=gg[:],
-                in0=g_sb[:, t, :, g * VC : (g + 1) * VC].unsqueeze(3).to_broadcast([P, J, VC, E]),
-                in1=gate_sb[:, t, :, 0:E].unsqueeze(2).to_broadcast([P, J, VC, E]),
+                out=gg[:, 0:jv],
+                in0=g_sb[:, t, 0:jv, g * VC : (g + 1) * VC].unsqueeze(3).to_broadcast([P, jv, VC, E]),
+                in1=gates[:, t, 0:jv, 0:E].unsqueeze(2).to_broadcast([P, jv, VC, E]),
                 op=ALU.mult,
             )
+            gg_tiles[i] = gg
+
+        def make_dz(i):
+            gg = gg_tiles.pop(i)
             dz = work.tile([P, J, KP], BF16, name="dz")
             nc.vector.scalar_tensor_tensor(
                 out=dz[:].rearrange("p j k -> p (j k)"),
@@ -139,12 +170,13 @@ def tile_plelayer_pb_v_kernel(
             )
             dz_tiles[i] = dz
 
-        def relayout(i):
-            dz = dz_tiles.pop(i)
-            dzi = work.tile([P, KP, J], BF16, name="dzi", align_bytes=64)
-            nc.scalar.copy(out=dzi[:], in_=dz[:].rearrange("p j k -> p k j"))
-            dzi_tiles[i] = dzi
-            words = dz[:].rearrange("p j k -> p (j k)").bitcast(F32)
+        def interleave(i, eng, lo, hi):
+            if i not in dzi_tiles:
+                dzi_tiles[i] = work.tile([P, KP, J], BF16, name="dzi", align_bytes=64)
+            copy_on(eng, dzi_tiles[i][:, lo:hi, :], dz_tiles[i][:, :, lo:hi].rearrange("p j k -> p k j"))
+
+        def turn(i):
+            words = dz_tiles[i][:].rearrange("p j k -> p (j k)").bitcast(F32)
             dzt = work.tile([P, B * J], BF16, name="dzt", align_bytes=64)
             dzt_w = dzt[:].bitcast(F32)
             for hb in range(2):
@@ -160,21 +192,25 @@ def tile_plelayer_pb_v_kernel(
                 )
             dzt_tiles[i] = dzt
 
-        def quant(i):
+        def quant_dw(i):
             ci = work.tile([P, KP], U32, name="ci", align_bytes=64)
             si = work.tile([P, KP], U8, name="si", align_bytes=64)
             nc.vector.quantize_mx(
                 out=ci[:].bitcast(E5), scales=si[:], in_=dzi_tiles.pop(i)[:].rearrange("p k j -> p (k j)")
             )
+            qi_tiles[i] = (ci, si)
+
+        def quant_dx(i):
             ct = work.tile([P, B], U32, name="ct", align_bytes=64)
             stl = work.tile([P, B], U8, name="stl", align_bytes=64)
             nc.vector.quantize_mx(out=ct[:].bitcast(E5), scales=stl[:], in_=dzt_tiles.pop(i)[:])
-            q_tiles[i] = (ci, si, ct, stl)
+            qt_tiles[i] = (ct, stl)
 
-        def multiply(i):
+        dw_ps = {}
+
+        def mult_dw(i):
             t, g = chunks[i]
-            ci, si, ct, stl = q_tiles.pop(i)
-            dw_sb = work.tile([P, UB, KP], F32, name="dw_sb")
+            ci, si = qi_tiles.pop(i)
             for ub in range(UB):
                 cols = slice(ub * P, (ub + 1) * P)
                 ps = dwp.tile([P, KP], F32, name="dwps")
@@ -187,15 +223,25 @@ def tile_plelayer_pb_v_kernel(
                     start=True,
                     stop=True,
                 )
-                nc.scalar.copy(out=dw_sb[:, ub, :], in_=ps[:])
+                dw_ps[(i, ub)] = ps
+
+        def store_dw(i, engs):
+            t, g = chunks[i]
+            dw_sb = work.tile([P, UB, KP], F32, name="dw_sb")
+            for ub in range(UB):
+                copy_on(engs[ub], dw_sb[:, ub, :], dw_ps.pop((i, ub))[:])
             dst = out_1[t].rearrange("(ub p) v e -> p ub (v e)", p=P)
             nc.sync.dma_start(out=dst[:, :, g * KP : (g + 1) * KP], in_=dw_sb[:])
+
+        def mult_dx(i):
+            t, g = chunks[i]
+            ct, stl = qt_tiles.pop(i)
             for ub in range(UB):
                 cols = slice(ub * P, (ub + 1) * P)
                 if g == 0:
-                    acc[ub] = accp.tile([P, B], F32, name="acc%d" % ub)
+                    acc[(t, ub)] = accp.tile([P, B], F32, name="acc%d" % ub)
                 nc.tensor.matmul_mx(
-                    out=acc[ub][:],
+                    out=acc[(t, ub)][:],
                     lhsT=w_codes[:, t, g, cols].bitcast(E4),
                     lhsT_scale=w_scales[:, t, g, cols],
                     rhs=ct[:].bitcast(E5),
@@ -203,38 +249,101 @@ def tile_plelayer_pb_v_kernel(
                     start=(g == 0),
                     stop=(g == NG - 1),
                 )
-            if g == NG - 1:
-                finish_dx(t)
 
-        def finish_dx(t):
-            dxt = two.tile([P, UB, B], F32, name="dxt")
-            for ub in range(UB):
-                nc.scalar.copy(out=dxt[:, ub, :], in_=acc[ub][:])
-            dx_sb = two.tile([P, J, U], F32, name="dx_sb")
-            for hb in range(2):
-                xt = tpp.tile([P, 2, UB, P], F32, name="tp")
-                for jj in range(2):
-                    j = 2 * hb + jj
-                    for ub in range(UB):
-                        nc.tensor.transpose(xt[:, jj, ub, :], dxt[:, ub, j * P : (j + 1) * P], ident[:])
-                nc.scalar.copy(
-                    out=dx_sb[:, 2 * hb : 2 * hb + 2, :].rearrange("p j u -> p (j u)"),
-                    in_=xt[:].rearrange("p j ub r -> p (j ub r)"),
-                )
-            nc.sync.dma_start(out=out_0[t].rearrange("(p j) u -> p j u", j=J), in_=dx_sb[:])
+        dx_parts = {}
 
-        w_transpose(0)
-        for i in range(n + 1):
-            if i < n:
-                make_dz(i)
-                if i + 6 < n:
-                    load_zt(i + 6)
-                relayout(i)
-                if i + 1 < n:
-                    w_transpose(i + 1)
+        def dx_out(t, ub, eng):
+            if t not in dx_parts:
+                dxt_new = two.tile([P, UB, B], F32, name="dxt")
+                dx_new = two.tile([P, J, U], F32, name="dx_sb")
+                dx_parts[t] = (dxt_new, dx_new)
+            copy_on(eng, dx_parts[t][0][:, ub, :], acc.pop((t, ub))[:])
+
+        dx_ps = {}
+
+        def dx_turn(t, hb):
+            dxt = dx_parts[t][0]
+            xt = tpp.tile([P, 2, UB, P], F32, name="tp")
+            for jj in range(2):
+                j = 2 * hb + jj
+                for ub in range(UB):
+                    nc.tensor.transpose(xt[:, jj, ub, :], dxt[:, ub, j * P : (j + 1) * P], ident[:])
+            dx_ps[(t, hb)] = xt
+
+        def dx_back(t, hb, eng):
+            copy_on(
+                eng,
+                dx_parts[t][1][:, 2 * hb : 2 * hb + 2, :].rearrange("p j u -> p (j u)"),
+                dx_ps.pop((t, hb))[:].rearrange("p j ub r -> p (j ub r)"),
+            )
+
+        def dx_store(t):
+            nc.sync.dma_start(out=out_0[t].rearrange("(p j) u -> p j u", j=J), in_=dx_parts[t][1][:])
+
+        def dx_half(t, hb):
+            dx_turn(t, hb)
+            dx_back(t, hb, "s")
+            if hb == 1:
+                dx_store(t)
+
+        make_gg(0)
+        for i in range(n):
+            make_dz(i)
             if i >= 1:
-                quant(i - 1)
-            if i < n:
+                quant_dw(i - 1)
+            if i + 1 < n:
+                make_gg(i + 1)
+            if i + ZB < n:
+                load_zt(i + ZB)
+            if i % 2 == 0 and i // 2 + 2 < n // 2:
+                load_w(i // 2 + 2)
+            if i < last:
+                interleave(i, "s", 0, KP)
+                turn(i)
+            else:
+                turn(i)
+                interleave(i, "s", 0, KP // 2)
+            if i == 0:
+                w_transpose(0)
+                for t in range(T):
+                    h_grp = two.tile([P, U, J], BF16, name="h_grp", align_bytes=64)
+                    nc.scalar.copy(out=h_grp[:], in_=h_sb[:, t].rearrange("p j u -> p u j"))
+                    h_grps.append(h_grp)
+            if i + 1 < n:
+                w_transpose(i + 1)
+            if i >= 1:
+                quant_dx(i - 1)
+            if i == 1:
+                w_quant(0)
+                for t in range(T):
+                    nc.vector.quantize_mx(
+                        out=h_codes[:, t, :].bitcast(E4),
+                        scales=h_scales[:, t, :],
+                        in_=h_grps[t][:].rearrange("p u j -> p (u j)"),
+                    )
+            if i >= 1:
                 w_quant(i)
-            if i >= 1:
-                multiply(i - 1)
+                mult_dw(i - 1)
+                mult_dx(i - 1)
+                store_dw(i - 1, "ss")
+                if chunks[i - 1] == (0, NG - 1):
+                    dx_out(0, 0, "s")
+                    dx_out(0, 1, "s")
+                    pending.append(lambda: dx_half(0, 0))
+                    pending.append(lambda: dx_half(0, 1))
+                elif pending:
+                    pending.pop(0)()
+
+        interleave(last, "v", KP // 2, KP)
+        quant_dx(last)
+        mult_dx(last)
+        quant_dw(last)
+        mult_dw(last)
+        dx_out(1, 0, "s")
+        dx_out(1, 1, "v")
+        dx_turn(1, 0)
+        dx_turn(1, 1)
+        store_dw(last, "sv")
+        dx_back(1, 0, "s")
+        dx_back(1, 1, "v")
+        dx_store(1)

@@ -173,7 +173,11 @@ def tile_plelayer_pb_v_kernel(
         def interleave(i, eng, lo, hi):
             if i not in dzi_tiles:
                 dzi_tiles[i] = work.tile([P, KP, J], BF16, name="dzi", align_bytes=64)
-            copy_on(eng, dzi_tiles[i][:, lo:hi, :], dz_tiles[i][:, :, lo:hi].rearrange("p j k -> p k j"))
+            copy_on(
+                eng,
+                dzi_tiles[i][:, lo:hi, :].rearrange("p (c q) j -> p c j q", q=4),
+                dz_tiles[i][:, :, lo:hi].rearrange("p j (c q) -> p c j q", q=4),
+            )
 
         def turn(i):
             words = dz_tiles[i][:].rearrange("p j k -> p (j k)").bitcast(F32)

@@ -24,7 +24,9 @@ NG = K // KP
 VC = KP // E
 UB = U // P
 ZB = 6
-GJ = 1
+JV = 2
+EARLY = 4
+VDW_EVERY = 1000
 
 
 def tile_plelayer_pb_v_kernel(
@@ -43,12 +45,14 @@ def tile_plelayer_pb_v_kernel(
         one = ctx.enter_context(tc.tile_pool(name="one", bufs=1))
         gatep = ctx.enter_context(tc.psum_pool(name="gatep", bufs=1))
         accp = ctx.enter_context(tc.psum_pool(name="accp", bufs=1))
-        tpp = ctx.enter_context(tc.psum_pool(name="tpp", bufs=3))
+        tpp = ctx.enter_context(tc.psum_pool(name="tpp", bufs=2))
         dwp = ctx.enter_context(tc.psum_pool(name="dwp", bufs=2))
         ctx.enter_context(tc.manual_schedule())
 
         ident = const.tile([P, P], F32, name="ident")
         make_identity(nc, ident[:])
+        ident_b = const.tile([P, P], BF16, name="ident_b")
+        make_identity(nc, ident_b[:])
 
         def copy_on(eng, out, in_):
             if eng == "v":
@@ -69,7 +73,12 @@ def tile_plelayer_pb_v_kernel(
             t, g = chunks[i]
             z = ztp.tile([P, J, KP], F32, name="z")
             src = zt[t].rearrange("(p j) v e -> p j (v e)", j=J)
-            nc.sync.dma_start(out=z[:], in_=src[:, :, g * KP : (g + 1) * KP])
+            if i == 0:
+                for half in range(2):
+                    js = slice(half * JV, (half + 1) * JV)
+                    nc.sync.dma_start(out=z[:, js, :], in_=src[:, js, g * KP : (g + 1) * KP])
+            else:
+                nc.sync.dma_start(out=z[:], in_=src[:, :, g * KP : (g + 1) * KP])
             zt_tiles[i] = z
 
         w_tiles = {}
@@ -99,6 +108,22 @@ def tile_plelayer_pb_v_kernel(
         nc.scalar.copy(out=gate_t[:], in_=gt_ps[:])
         gate_ps = gatep.tile([P, T, J, G16], F32, name="gate_ps")
         nc.tensor.transpose(gate_ps[:].rearrange("p t j g -> p (t j g)"), gate_t[:], ident[:])
+
+        g_t = const.tile([P, T, NG // 2, JV, P], BF16, name="g_t")
+        g_ps = gatep.tile([P, NG, JV, VC], BF16, name="g_ps")
+
+        def g_turn(t):
+            t1 = tpp.tile([P, NG // 2, JV, P], BF16, name="tp")
+            for b in range(NG // 2):
+                for j in range(JV):
+                    nc.tensor.transpose(t1[:, b, j, :], g_sb[:, t, j, b * P : (b + 1) * P], ident_b[:])
+            nc.scalar.copy(
+                out=g_t[:, t].rearrange("p b j r -> p (b j r)"), in_=t1[:].rearrange("p b j r -> p (b j r)")
+            )
+
+        def g_back(t, b):
+            for j in range(JV):
+                nc.tensor.transpose(g_ps[:, 2 * b : 2 * b + 2, j, :], g_t[:, t, b, j, :], ident_b[:])
 
         h_codes = const.tile([P, T, U], U32, name="h_codes", align_bytes=64)
         h_scales = const.tile([P, T, U], U8, name="h_scales", align_bytes=64)
@@ -136,39 +161,65 @@ def tile_plelayer_pb_v_kernel(
         pending = []
 
         gg_tiles = {}
+        m1_tiles = {}
 
         def make_gg(i):
             t, g = chunks[i]
-            gg = one.tile([P, J, VC, E], F32, name="gg")
-            jv = J - GJ
-            gates = gate_sb if i == 0 else gate_ps
-            if GJ > 0:
-                nc.gpsimd.tensor_tensor(
-                    out=gg[:, jv:J],
-                    in0=g_sb[:, t, jv:J, g * VC : (g + 1) * VC].unsqueeze(3).to_broadcast([P, GJ, VC, E]),
-                    in1=gate_sb[:, t, jv:J, 0:E].unsqueeze(2).to_broadcast([P, GJ, VC, E]),
-                    op=ALU.mult,
-                )
-            nc.vector.tensor_tensor(
-                out=gg[:, 0:jv],
-                in0=g_sb[:, t, 0:jv, g * VC : (g + 1) * VC].unsqueeze(3).to_broadcast([P, jv, VC, E]),
-                in1=gates[:, t, 0:jv, 0:E].unsqueeze(2).to_broadcast([P, jv, VC, E]),
+            gg = one.tile([P, J - JV, VC, E], F32, name="gg")
+            nc.gpsimd.tensor_tensor(
+                out=gg[:],
+                in0=g_sb[:, t, JV:J, g * VC : (g + 1) * VC].unsqueeze(3).to_broadcast([P, J - JV, VC, E]),
+                in1=gate_sb[:, t, JV:J, 0:E].unsqueeze(2).to_broadcast([P, J - JV, VC, E]),
                 op=ALU.mult,
             )
             gg_tiles[i] = gg
 
-        def make_dz(i):
-            gg = gg_tiles.pop(i)
+        def mask_g(i):
+            t, g = chunks[i]
+            m1 = two.tile([P, JV, VC, E], BF16, name="m1")
+            z = zt_tiles[i]
+            if i < EARLY:
+                for j in range(JV):
+                    nc.vector.scalar_tensor_tensor(
+                        out=m1[:, j].rearrange("p v e -> p (v e)"),
+                        in0=z[:, j, :],
+                        scalar=0.0,
+                        in1=g_sb[:, t, j, g * VC : (g + 1) * VC].unsqueeze(2).to_broadcast([P, VC, E]),
+                        op0=ALU.is_gt,
+                        op1=ALU.mult,
+                    )
+            else:
+                nc.vector.scalar_tensor_tensor(
+                    out=m1[:].rearrange("p j v e -> p (j v e)"),
+                    in0=z[:, 0:JV, :].rearrange("p j k -> p (j k)"),
+                    scalar=0.0,
+                    in1=g_ps[:, g].rearrange("p j v -> p (j v)").unsqueeze(2).to_broadcast([P, JV * VC, E]),
+                    op0=ALU.is_gt,
+                    op1=ALU.mult,
+                )
+            m1_tiles[i] = m1
+
+        def times_gate(i):
+            t, g = chunks[i]
+            gates = gate_sb if i < EARLY else gate_ps
             dz = work.tile([P, J, KP], BF16, name="dz")
+            nc.vector.tensor_tensor(
+                out=dz[:, 0:JV, :].rearrange("p j (v e) -> p j v e", e=E),
+                in0=m1_tiles.pop(i)[:],
+                in1=gates[:, t, 0:JV, 0:E].unsqueeze(2).to_broadcast([P, JV, VC, E]),
+                op=ALU.mult,
+            )
+            dz_tiles[i] = dz
+
+        def mask_gg(i):
             nc.vector.scalar_tensor_tensor(
-                out=dz[:].rearrange("p j k -> p (j k)"),
-                in0=zt_tiles.pop(i)[:].rearrange("p j k -> p (j k)"),
+                out=dz_tiles[i][:, JV:J, :].rearrange("p j k -> p (j k)"),
+                in0=zt_tiles.pop(i)[:, JV:J, :].rearrange("p j k -> p (j k)"),
                 scalar=0.0,
-                in1=gg[:].rearrange("p j v e -> p (j v e)"),
+                in1=gg_tiles.pop(i)[:].rearrange("p j v e -> p (j v e)"),
                 op0=ALU.is_gt,
                 op1=ALU.mult,
             )
-            dz_tiles[i] = dz
 
         def interleave(i, eng, lo, hi):
             if i not in dzi_tiles:
@@ -291,16 +342,28 @@ def tile_plelayer_pb_v_kernel(
                 dx_store(t)
 
         make_gg(0)
+        mask_g(0)
+        times_gate(0)
+        g_turn(0)
+        for b in range(NG // 2):
+            g_back(0, b)
         for i in range(n):
-            make_dz(i)
+            mask_gg(i)
             if i >= 1:
                 quant_dw(i - 1)
+            if i == 0:
+                mask_g(1)
             if i + 1 < n:
                 make_gg(i + 1)
+                times_gate(i + 1)
+            if i + 2 < n:
+                mask_g(i + 2)
             if i + ZB < n:
                 load_zt(i + ZB)
             if i % 2 == 0 and i // 2 + 2 < n // 2:
                 load_w(i // 2 + 2)
+            if 1 <= i < last:
+                w_transpose(i + 1)
             if i < last:
                 interleave(i, "s", 0, KP)
                 turn(i)
@@ -313,8 +376,7 @@ def tile_plelayer_pb_v_kernel(
                     h_grp = two.tile([P, U, J], BF16, name="h_grp", align_bytes=64)
                     nc.scalar.copy(out=h_grp[:], in_=h_sb[:, t].rearrange("p j u -> p u j"))
                     h_grps.append(h_grp)
-            if i + 1 < n:
-                w_transpose(i + 1)
+                w_transpose(1)
             if i >= 1:
                 quant_dx(i - 1)
             if i == 1:
@@ -329,7 +391,11 @@ def tile_plelayer_pb_v_kernel(
                 w_quant(i)
                 mult_dw(i - 1)
                 mult_dx(i - 1)
-                store_dw(i - 1, "ss")
+                store_dw(i - 1, "sv" if (i % VDW_EVERY == 0) else "ss")
+                if i == 3:
+                    g_turn(1)
+                if i in (5, 7, 9, 11):
+                    g_back(1, (i - 5) // 2)
                 if chunks[i - 1] == (0, NG - 1):
                     dx_out(0, 0, "s")
                     dx_out(0, 1, "s")

@@ -24,9 +24,7 @@ NG = K // KP
 VC = KP // E
 UB = U // P
 ZB = 6
-JV = 2
-EARLY = 4
-VDW_EVERY = 1000
+GJ = 1
 
 
 def tile_plelayer_pb_v_kernel(
@@ -45,14 +43,12 @@ def tile_plelayer_pb_v_kernel(
         one = ctx.enter_context(tc.tile_pool(name="one", bufs=1))
         gatep = ctx.enter_context(tc.psum_pool(name="gatep", bufs=1))
         accp = ctx.enter_context(tc.psum_pool(name="accp", bufs=1))
-        tpp = ctx.enter_context(tc.psum_pool(name="tpp", bufs=2))
+        tpp = ctx.enter_context(tc.psum_pool(name="tpp", bufs=3))
         dwp = ctx.enter_context(tc.psum_pool(name="dwp", bufs=2))
         ctx.enter_context(tc.manual_schedule())
 
         ident = const.tile([P, P], F32, name="ident")
         make_identity(nc, ident[:])
-        ident_b = const.tile([P, P], BF16, name="ident_b")
-        make_identity(nc, ident_b[:])
 
         def copy_on(eng, out, in_):
             if eng == "v":
@@ -73,12 +69,7 @@ def tile_plelayer_pb_v_kernel(
             t, g = chunks[i]
             z = ztp.tile([P, J, KP], F32, name="z")
             src = zt[t].rearrange("(p j) v e -> p j (v e)", j=J)
-            if i == 0:
-                for half in range(2):
-                    js = slice(half * JV, (half + 1) * JV)
-                    nc.sync.dma_start(out=z[:, js, :], in_=src[:, js, g * KP : (g + 1) * KP])
-            else:
-                nc.sync.dma_start(out=z[:], in_=src[:, :, g * KP : (g + 1) * KP])
+            nc.sync.dma_start(out=z[:], in_=src[:, :, g * KP : (g + 1) * KP])
             zt_tiles[i] = z
 
         w_tiles = {}
@@ -109,22 +100,6 @@ def tile_plelayer_pb_v_kernel(
         gate_ps = gatep.tile([P, T, J, G16], F32, name="gate_ps")
         nc.tensor.transpose(gate_ps[:].rearrange("p t j g -> p (t j g)"), gate_t[:], ident[:])
 
-        g_t = const.tile([P, T, NG // 2, JV, P], BF16, name="g_t")
-        g_ps = gatep.tile([P, NG, JV, VC], BF16, name="g_ps")
-
-        def g_turn(t):
-            t1 = tpp.tile([P, NG // 2, JV, P], BF16, name="tp")
-            for b in range(NG // 2):
-                for j in range(JV):
-                    nc.tensor.transpose(t1[:, b, j, :], g_sb[:, t, j, b * P : (b + 1) * P], ident_b[:])
-            nc.scalar.copy(
-                out=g_t[:, t].rearrange("p b j r -> p (b j r)"), in_=t1[:].rearrange("p b j r -> p (b j r)")
-            )
-
-        def g_back(t, b):
-            for j in range(JV):
-                nc.tensor.transpose(g_ps[:, 2 * b : 2 * b + 2, j, :], g_t[:, t, b, j, :], ident_b[:])
-
         h_codes = const.tile([P, T, U], U32, name="h_codes", align_bytes=64)
         h_scales = const.tile([P, T, U], U8, name="h_scales", align_bytes=64)
         h_grps = []
@@ -139,17 +114,20 @@ def tile_plelayer_pb_v_kernel(
                 for u in range(2):
                     lo = ub * KP + (i % 2) * (KP // 2)
                     nc.tensor.transpose(wt[:, ub, u, :], words[:, lo + u : lo + KP // 2 : 2], ident[:])
-            w_grp = work.tile([P, U * J], BF16, name="w_grp", align_bytes=64)
+            if i % 2 == 0:
+                w_grps[i // 2] = work.tile([P, 2 * U * J], BF16, name="w_grp", align_bytes=64)
+            half = w_grps[i // 2][:, (i % 2) * U * J : (i % 2 + 1) * U * J]
             nc.scalar.copy(
-                out=w_grp[:].bitcast(F32).rearrange("p (ub r u) -> p ub r u", ub=UB, u=2),
+                out=half.bitcast(F32).rearrange("p (ub r u) -> p ub r u", ub=UB, u=2),
                 in_=wt[:].rearrange("p ub u r -> p ub r u"),
             )
-            w_grps[i] = w_grp
 
-        def w_quant(i):
-            t, g = chunks[i]
+        def w_quant(q):
+            t, g = chunks[2 * q]
             nc.vector.quantize_mx(
-                out=w_codes[:, t, g, :].bitcast(E4), scales=w_scales[:, t, g, :], in_=w_grps.pop(i)[:]
+                out=w_codes[:, t, g : g + 2, :].rearrange("p g u -> p (g u)").bitcast(E4),
+                scales=w_scales[:, t, g : g + 2, :].rearrange("p g u -> p (g u)"),
+                in_=w_grps.pop(q)[:],
             )
 
         dz_tiles = {}
@@ -161,65 +139,39 @@ def tile_plelayer_pb_v_kernel(
         pending = []
 
         gg_tiles = {}
-        m1_tiles = {}
 
         def make_gg(i):
             t, g = chunks[i]
-            gg = one.tile([P, J - JV, VC, E], F32, name="gg")
-            nc.gpsimd.tensor_tensor(
-                out=gg[:],
-                in0=g_sb[:, t, JV:J, g * VC : (g + 1) * VC].unsqueeze(3).to_broadcast([P, J - JV, VC, E]),
-                in1=gate_sb[:, t, JV:J, 0:E].unsqueeze(2).to_broadcast([P, J - JV, VC, E]),
+            gg = one.tile([P, J, VC, E], F32, name="gg")
+            jv = J - GJ
+            gates = gate_sb if i == 0 else gate_ps
+            if GJ > 0:
+                nc.gpsimd.tensor_tensor(
+                    out=gg[:, jv:J],
+                    in0=g_sb[:, t, jv:J, g * VC : (g + 1) * VC].unsqueeze(3).to_broadcast([P, GJ, VC, E]),
+                    in1=gate_sb[:, t, jv:J, 0:E].unsqueeze(2).to_broadcast([P, GJ, VC, E]),
+                    op=ALU.mult,
+                )
+            nc.vector.tensor_tensor(
+                out=gg[:, 0:jv],
+                in0=g_sb[:, t, 0:jv, g * VC : (g + 1) * VC].unsqueeze(3).to_broadcast([P, jv, VC, E]),
+                in1=gates[:, t, 0:jv, 0:E].unsqueeze(2).to_broadcast([P, jv, VC, E]),
                 op=ALU.mult,
             )
             gg_tiles[i] = gg
 
-        def mask_g(i):
-            t, g = chunks[i]
-            m1 = two.tile([P, JV, VC, E], BF16, name="m1")
-            z = zt_tiles[i]
-            if i < EARLY:
-                for j in range(JV):
-                    nc.vector.scalar_tensor_tensor(
-                        out=m1[:, j].rearrange("p v e -> p (v e)"),
-                        in0=z[:, j, :],
-                        scalar=0.0,
-                        in1=g_sb[:, t, j, g * VC : (g + 1) * VC].unsqueeze(2).to_broadcast([P, VC, E]),
-                        op0=ALU.is_gt,
-                        op1=ALU.mult,
-                    )
-            else:
-                nc.vector.scalar_tensor_tensor(
-                    out=m1[:].rearrange("p j v e -> p (j v e)"),
-                    in0=z[:, 0:JV, :].rearrange("p j k -> p (j k)"),
-                    scalar=0.0,
-                    in1=g_ps[:, g].rearrange("p j v -> p (j v)").unsqueeze(2).to_broadcast([P, JV * VC, E]),
-                    op0=ALU.is_gt,
-                    op1=ALU.mult,
-                )
-            m1_tiles[i] = m1
-
-        def times_gate(i):
-            t, g = chunks[i]
-            gates = gate_sb if i < EARLY else gate_ps
+        def make_dz(i):
+            gg = gg_tiles.pop(i)
             dz = work.tile([P, J, KP], BF16, name="dz")
-            nc.vector.tensor_tensor(
-                out=dz[:, 0:JV, :].rearrange("p j (v e) -> p j v e", e=E),
-                in0=m1_tiles.pop(i)[:],
-                in1=gates[:, t, 0:JV, 0:E].unsqueeze(2).to_broadcast([P, JV, VC, E]),
-                op=ALU.mult,
-            )
-            dz_tiles[i] = dz
-
-        def mask_gg(i):
             nc.vector.scalar_tensor_tensor(
-                out=dz_tiles[i][:, JV:J, :].rearrange("p j k -> p (j k)"),
-                in0=zt_tiles.pop(i)[:, JV:J, :].rearrange("p j k -> p (j k)"),
+                out=dz[:].rearrange("p j k -> p (j k)"),
+                in0=zt_tiles.pop(i)[:].rearrange("p j k -> p (j k)"),
                 scalar=0.0,
-                in1=gg_tiles.pop(i)[:].rearrange("p j v e -> p (j v e)"),
+                in1=gg[:].rearrange("p j v e -> p (j v e)"),
                 op0=ALU.is_gt,
                 op1=ALU.mult,
             )
+            dz_tiles[i] = dz
 
         def interleave(i, eng, lo, hi):
             if i not in dzi_tiles:
@@ -283,10 +235,13 @@ def tile_plelayer_pb_v_kernel(
         def store_dw(i, engs):
             t, g = chunks[i]
             dw_sb = work.tile([P, UB, KP], F32, name="dw_sb")
+            dst = out_1[t].rearrange("(ub p) v e -> p ub (v e)", p=P)
             for ub in range(UB):
                 copy_on(engs[ub], dw_sb[:, ub, :], dw_ps.pop((i, ub))[:])
-            dst = out_1[t].rearrange("(ub p) v e -> p ub (v e)", p=P)
-            nc.sync.dma_start(out=dst[:, :, g * KP : (g + 1) * KP], in_=dw_sb[:])
+                if i == last:
+                    nc.sync.dma_start(out=dst[:, ub, g * KP : (g + 1) * KP], in_=dw_sb[:, ub, :])
+            if i < last:
+                nc.sync.dma_start(out=dst[:, :, g * KP : (g + 1) * KP], in_=dw_sb[:])
 
         def mult_dx(i):
             t, g = chunks[i]
@@ -342,28 +297,16 @@ def tile_plelayer_pb_v_kernel(
                 dx_store(t)
 
         make_gg(0)
-        mask_g(0)
-        times_gate(0)
-        g_turn(0)
-        for b in range(NG // 2):
-            g_back(0, b)
         for i in range(n):
-            mask_gg(i)
+            make_dz(i)
             if i >= 1:
                 quant_dw(i - 1)
-            if i == 0:
-                mask_g(1)
             if i + 1 < n:
                 make_gg(i + 1)
-                times_gate(i + 1)
-            if i + 2 < n:
-                mask_g(i + 2)
             if i + ZB < n:
                 load_zt(i + ZB)
             if i % 2 == 0 and i // 2 + 2 < n // 2:
                 load_w(i // 2 + 2)
-            if 1 <= i < last:
-                w_transpose(i + 1)
             if i < last:
                 interleave(i, "s", 0, KP)
                 turn(i)
@@ -374,28 +317,28 @@ def tile_plelayer_pb_v_kernel(
                 w_transpose(0)
                 for t in range(T):
                     h_grp = two.tile([P, U, J], BF16, name="h_grp", align_bytes=64)
-                    nc.scalar.copy(out=h_grp[:], in_=h_sb[:, t].rearrange("p j u -> p u j"))
+                    nc.scalar.copy(
+                        out=h_grp[:].rearrange("p (c q) j -> p c j q", q=4),
+                        in_=h_sb[:, t].rearrange("p j (c q) -> p c j q", q=4),
+                    )
                     h_grps.append(h_grp)
-                w_transpose(1)
+            if i + 1 < n:
+                w_transpose(i + 1)
             if i >= 1:
                 quant_dx(i - 1)
             if i == 1:
-                w_quant(0)
                 for t in range(T):
                     nc.vector.quantize_mx(
                         out=h_codes[:, t, :].bitcast(E4),
                         scales=h_scales[:, t, :],
                         in_=h_grps[t][:].rearrange("p u j -> p (u j)"),
                     )
+            if i % 2 == 1:
+                w_quant(i // 2)
             if i >= 1:
-                w_quant(i)
                 mult_dw(i - 1)
                 mult_dx(i - 1)
-                store_dw(i - 1, "sv" if (i % VDW_EVERY == 0) else "ss")
-                if i == 3:
-                    g_turn(1)
-                if i in (5, 7, 9, 11):
-                    g_back(1, (i - 5) // 2)
+                store_dw(i - 1, "ss")
                 if chunks[i - 1] == (0, NG - 1):
                     dx_out(0, 0, "s")
                     dx_out(0, 1, "s")
@@ -414,6 +357,8 @@ def tile_plelayer_pb_v_kernel(
         dx_turn(1, 0)
         dx_turn(1, 1)
         store_dw(last, "sv")
+        dx_dst = out_0[1].rearrange("(p j) u -> p j u", j=J)
         dx_back(1, 0, "s")
+        nc.scalar.dma_start(out=dx_dst[:, 0:2, :], in_=dx_parts[1][1][:, 0:2, :])
         dx_back(1, 1, "v")
-        dx_store(1)
+        nc.sync.dma_start(out=dx_dst[:, 2:4, :], in_=dx_parts[1][1][:, 2:4, :])

from contextlib import ExitStack

import concourse.mybir as mybir
from concourse.masks import make_identity

T, B, U, V, E = 2, 512, 256, 512, 8
G16 = 16
K = V * E
FLOPS = 2 * (2 * T * B * K * U)
BYTES = T * B * U * 2 + T * U * K * 2 + T * B * K * 4 + T * B * G16 * 4 + T * B * V * 2 + T * B * U * 4 + T * U * K * 4

F32 = mybir.dt.float32
BF16 = mybir.dt.bfloat16
U32 = mybir.dt.uint32
U8 = mybir.dt.uint8
E4 = mybir.dt.float8_e4m3fn_x4
E5 = mybir.dt.float8_e5m2_x4
ALU = mybir.AluOpType

P = 128
J = 4
KP = 512
NG = K // KP
VC = KP // E
UB = U // P
ZB = 6
GJ = 1


def tile_plelayer_pb_v_kernel(
    tc, task_h, share_h, ews1, ebs1, ew1, eb1, gate_pre1, gb1, zt, gate, grad_out, out_0, out_1
):
    nc = tc.nc
    chunks = [(t, g) for t in range(T) for g in range(NG)]
    n = len(chunks)
    last = n - 1

    with ExitStack() as ctx:
        const = ctx.enter_context(tc.tile_pool(name="const", bufs=1))
        ztp = ctx.enter_context(tc.tile_pool(name="ztp", bufs=ZB))
        work = ctx.enter_context(tc.tile_pool(name="work", bufs=3))
        two = ctx.enter_context(tc.tile_pool(name="two", bufs=2))
        one = ctx.enter_context(tc.tile_pool(name="one", bufs=1))
        gatep = ctx.enter_context(tc.psum_pool(name="gatep", bufs=1))
        accp = ctx.enter_context(tc.psum_pool(name="accp", bufs=1))
        tpp = ctx.enter_context(tc.psum_pool(name="tpp", bufs=3))
        dwp = ctx.enter_context(tc.psum_pool(name="dwp", bufs=2))
        ctx.enter_context(tc.manual_schedule())

        ident = const.tile([P, P], F32, name="ident")
        make_identity(nc, ident[:])

        def copy_on(eng, out, in_):
            if eng == "v":
                nc.vector.tensor_copy(out=out, in_=in_)
            else:
                nc.scalar.copy(out=out, in_=in_)

        gate_sb = const.tile([P, T, J, G16], F32, name="gate_sb")
        nc.sync.dma_start(out=gate_sb[:], in_=gate.rearrange("t (p j) g -> p t j g", j=J))
        g_sb = const.tile([P, T, J, V], BF16, name="g_sb")
        h_sb = const.tile([P, T, J, U], BF16, name="h_sb")
        g_src = grad_out.rearrange("t (p j) v -> p t j v", j=J)
        nc.sync.dma_start(out=g_sb[:, 0, :, 0 : 2 * VC], in_=g_src[:, 0, :, 0 : 2 * VC])

        zt_tiles = {}

        def load_zt(i):
            t, g = chunks[i]
            z = ztp.tile([P, J, KP], F32, name="z")
            src = zt[t].rearrange("(p j) v e -> p j (v e)", j=J)
            nc.sync.dma_start(out=z[:], in_=src[:, :, g * KP : (g + 1) * KP])
            zt_tiles[i] = z

        w_tiles = {}

        def load_w(q):
            t, pr = q // (NG // 2), q % (NG // 2)
            w_pair = const.tile([P, UB, 2 * KP], BF16, name="w_pair%d" % q)
            src = ew1[t].rearrange("(ub p) v e -> p ub (v e)", p=P)
            nc.sync.dma_start(out=w_pair[:], in_=src[:, :, pr * 2 * KP : (pr + 1) * 2 * KP])
            w_tiles[q] = w_pair

        load_zt(0)
        nc.sync.dma_start(out=g_sb[:, 0, :, 2 * VC : V], in_=g_src[:, 0, :, 2 * VC : V])
        load_zt(1)
        load_w(0)
        nc.sync.dma_start(out=h_sb[:], in_=task_h.rearrange("t (p j) u -> p t j u", j=J))
        load_zt(2)
        load_zt(3)
        load_w(1)
        load_zt(4)
        load_zt(5)
        nc.sync.dma_start(out=g_sb[:, 1], in_=g_src[:, 1])

        gt_ps = tpp.tile([P, P], F32, name="tp")
        nc.tensor.transpose(gt_ps[:], gate_sb[:].rearrange("p t j g -> p (t j g)"), ident[:])
        gate_t = const.tile([P, P], F32, name="gate_t")
        nc.scalar.copy(out=gate_t[:], in_=gt_ps[:])
        gate_ps = gatep.tile([P, T, J, G16], F32, name="gate_ps")
        nc.tensor.transpose(gate_ps[:].rearrange("p t j g -> p (t j g)"), gate_t[:], ident[:])

        h_codes = const.tile([P, T, U], U32, name="h_codes", align_bytes=64)
        h_scales = const.tile([P, T, U], U8, name="h_scales", align_bytes=64)
        h_grps = []
        w_codes = const.tile([P, T, NG, U], U32, name="w_codes", align_bytes=64)
        w_scales = const.tile([P, T, NG, U], U8, name="w_scales", align_bytes=64)
        w_grps = {}

        def w_transpose(i):
            words = w_tiles[i // 2][:].rearrange("p ub k -> p (ub k)").bitcast(F32)
            wt = tpp.tile([P, UB, 2, P], F32, name="tp")
            for ub in range(UB):
                for u in range(2):
                    lo = ub * KP + (i % 2) * (KP // 2)
                    nc.tensor.transpose(wt[:, ub, u, :], words[:, lo + u : lo + KP // 2 : 2], ident[:])
            if i % 2 == 0:
                w_grps[i // 2] = work.tile([P, 2 * U * J], BF16, name="w_grp", align_bytes=64)
            half = w_grps[i // 2][:, (i % 2) * U * J : (i % 2 + 1) * U * J]
            nc.scalar.copy(
                out=half.bitcast(F32).rearrange("p (ub r u) -> p ub r u", ub=UB, u=2),
                in_=wt[:].rearrange("p ub u r -> p ub r u"),
            )

        def w_quant(q):
            t, g = chunks[2 * q]
            nc.vector.quantize_mx(
                out=w_codes[:, t, g : g + 2, :].rearrange("p g u -> p (g u)").bitcast(E4),
                scales=w_scales[:, t, g : g + 2, :].rearrange("p g u -> p (g u)"),
                in_=w_grps.pop(q)[:],
            )

        dz_tiles = {}
        dzi_tiles = {}
        dzt_tiles = {}
        qi_tiles = {}
        qt_tiles = {}
        acc = {}
        pending = []

        gg_tiles = {}

        def make_gg(i):
            t, g = chunks[i]
            gg = one.tile([P, J, VC, E], F32, name="gg")
            jv = J - GJ
            gates = gate_sb if i == 0 else gate_ps
            if GJ > 0:
                nc.gpsimd.tensor_tensor(
                    out=gg[:, jv:J],
                    in0=g_sb[:, t, jv:J, g * VC : (g + 1) * VC].unsqueeze(3).to_broadcast([P, GJ, VC, E]),
                    in1=gate_sb[:, t, jv:J, 0:E].unsqueeze(2).to_broadcast([P, GJ, VC, E]),
                    op=ALU.mult,
                )
            nc.vector.tensor_tensor(
                out=gg[:, 0:jv],
                in0=g_sb[:, t, 0:jv, g * VC : (g + 1) * VC].unsqueeze(3).to_broadcast([P, jv, VC, E]),
                in1=gates[:, t, 0:jv, 0:E].unsqueeze(2).to_broadcast([P, jv, VC, E]),
                op=ALU.mult,
            )
            gg_tiles[i] = gg

        def make_dz(i):
            gg = gg_tiles.pop(i)
            dz = work.tile([P, J, KP], BF16, name="dz")
            nc.vector.scalar_tensor_tensor(
                out=dz[:].rearrange("p j k -> p (j k)"),
                in0=zt_tiles.pop(i)[:].rearrange("p j k -> p (j k)"),
                scalar=0.0,
                in1=gg[:].rearrange("p j v e -> p (j v e)"),
                op0=ALU.is_gt,
                op1=ALU.mult,
            )
            dz_tiles[i] = dz

        def interleave(i, eng, lo, hi):
            if i not in dzi_tiles:
                dzi_tiles[i] = work.tile([P, KP, J], BF16, name="dzi", align_bytes=64)
            copy_on(
                eng,
                dzi_tiles[i][:, lo:hi, :].rearrange("p (c q) j -> p c j q", q=4),
                dz_tiles[i][:, :, lo:hi].rearrange("p j (c q) -> p c j q", q=4),
            )

        def turn(i):
            words = dz_tiles[i][:].rearrange("p j k -> p (j k)").bitcast(F32)
            dzt = work.tile([P, B * J], BF16, name="dzt", align_bytes=64)
            dzt_w = dzt[:].bitcast(F32)
            for hb in range(2):
                xt = tpp.tile([P, 2, 2, P], F32, name="tp")
                for jj in range(2):
                    j = 2 * hb + jj
                    for u in range(2):
                        lo = j * (KP // 2)
                        nc.tensor.transpose(xt[:, jj, u, :], words[:, lo + u : lo + KP // 2 : 2], ident[:])
                nc.scalar.copy(
                    out=dzt_w[:, hb * 512 : (hb + 1) * 512].rearrange("p (j r u) -> p j r u", j=2, u=2),
                    in_=xt[:].rearrange("p j u r -> p j r u"),
                )
            dzt_tiles[i] = dzt

        def quant_dw(i):
            ci = work.tile([P, KP], U32, name="ci", align_bytes=64)
            si = work.tile([P, KP], U8, name="si", align_bytes=64)
            nc.vector.quantize_mx(
                out=ci[:].bitcast(E5), scales=si[:], in_=dzi_tiles.pop(i)[:].rearrange("p k j -> p (k j)")
            )
            qi_tiles[i] = (ci, si)

        def quant_dx(i):
            ct = work.tile([P, B], U32, name="ct", align_bytes=64)
            stl = work.tile([P, B], U8, name="stl", align_bytes=64)
            nc.vector.quantize_mx(out=ct[:].bitcast(E5), scales=stl[:], in_=dzt_tiles.pop(i)[:])
            qt_tiles[i] = (ct, stl)

        dw_ps = {}

        def mult_dw(i):
            t, g = chunks[i]
            ci, si = qi_tiles.pop(i)
            for ub in range(UB):
                cols = slice(ub * P, (ub + 1) * P)
                ps = dwp.tile([P, KP], F32, name="dwps")
                nc.tensor.matmul_mx(
                    out=ps[:],
                    lhsT=h_codes[:, t, cols].bitcast(E4),
                    lhsT_scale=h_scales[:, t, cols],
                    rhs=ci[:].bitcast(E5),
                    rhs_scale=si[:],
                    start=True,
                    stop=True,
                )
                dw_ps[(i, ub)] = ps

        def store_dw(i, engs):
            t, g = chunks[i]
            dw_sb = work.tile([P, UB, KP], F32, name="dw_sb")
            dst = out_1[t].rearrange("(ub p) v e -> p ub (v e)", p=P)
            for ub in range(UB):
                copy_on(engs[ub], dw_sb[:, ub, :], dw_ps.pop((i, ub))[:])
                if i == last:
                    nc.sync.dma_start(out=dst[:, ub, g * KP : (g + 1) * KP], in_=dw_sb[:, ub, :])
            if i < last:
                nc.sync.dma_start(out=dst[:, :, g * KP : (g + 1) * KP], in_=dw_sb[:])

        def mult_dx(i):
            t, g = chunks[i]
            ct, stl = qt_tiles.pop(i)
            for ub in range(UB):
                cols = slice(ub * P, (ub + 1) * P)
                if g == 0:
                    acc[(t, ub)] = accp.tile([P, B], F32, name="acc%d" % ub)
                nc.tensor.matmul_mx(
                    out=acc[(t, ub)][:],
                    lhsT=w_codes[:, t, g, cols].bitcast(E4),
                    lhsT_scale=w_scales[:, t, g, cols],
                    rhs=ct[:].bitcast(E5),
                    rhs_scale=stl[:],
                    start=(g == 0),
                    stop=(g == NG - 1),
                )

        dx_parts = {}

        def dx_out(t, ub, eng):
            if t not in dx_parts:
                dxt_new = two.tile([P, UB, B], F32, name="dxt")
                dx_new = two.tile([P, J, U], F32, name="dx_sb")
                dx_parts[t] = (dxt_new, dx_new)
            copy_on(eng, dx_parts[t][0][:, ub, :], acc.pop((t, ub))[:])

        dx_ps = {}

        def dx_turn(t, hb):
            dxt = dx_parts[t][0]
            xt = tpp.tile([P, 2, UB, P], F32, name="tp")
            for jj in range(2):
                j = 2 * hb + jj
                for ub in range(UB):
                    nc.tensor.transpose(xt[:, jj, ub, :], dxt[:, ub, j * P : (j + 1) * P], ident[:])
            dx_ps[(t, hb)] = xt

        def dx_back(t, hb, eng):
            copy_on(
                eng,
                dx_parts[t][1][:, 2 * hb : 2 * hb + 2, :].rearrange("p j u -> p (j u)"),
                dx_ps.pop((t, hb))[:].rearrange("p j ub r -> p (j ub r)"),
            )

        def dx_store(t):
            nc.sync.dma_start(out=out_0[t].rearrange("(p j) u -> p j u", j=J), in_=dx_parts[t][1][:])

        def dx_half(t, hb):
            dx_turn(t, hb)
            dx_back(t, hb, "s")
            if hb == 1:
                dx_store(t)

        make_gg(0)
        for i in range(n):
            make_dz(i)
            if i >= 1:
                quant_dw(i - 1)
            if i + 1 < n:
                make_gg(i + 1)
            if i + ZB < n:
                load_zt(i + ZB)
            if i % 2 == 0 and i // 2 + 2 < n // 2:
                load_w(i // 2 + 2)
            if i < last:
                interleave(i, "s", 0, KP)
                turn(i)
            else:
                turn(i)
                interleave(i, "s", 0, KP // 2)
            if i == 0:
                w_transpose(0)
                for t in range(T):
                    h_grp = two.tile([P, U, J], BF16, name="h_grp", align_bytes=64)
                    nc.scalar.copy(
                        out=h_grp[:].rearrange("p (c q) j -> p c j q", q=4),
                        in_=h_sb[:, t].rearrange("p j (c q) -> p c j q", q=4),
                    )
                    h_grps.append(h_grp)
            if i + 1 < n:
                w_transpose(i + 1)
            if i >= 1:
                quant_dx(i - 1)
            if i == 1:
                for t in range(T):
                    nc.vector.quantize_mx(
                        out=h_codes[:, t, :].bitcast(E4),
                        scales=h_scales[:, t, :],
                        in_=h_grps[t][:].rearrange("p u j -> p (u j)"),
                    )
            if i % 2 == 1:
                w_quant(i // 2)
            if i >= 1:
                mult_dw(i - 1)
                mult_dx(i - 1)
                store_dw(i - 1, "ss")
                if chunks[i - 1] == (0, NG - 1):
                    dx_out(0, 0, "s")
                    dx_out(0, 1, "s")
                    pending.append(lambda: dx_half(0, 0))
                    pending.append(lambda: dx_half(0, 1))
                elif pending:
                    pending.pop(0)()

        interleave(last, "v", KP // 2, KP)
        quant_dx(last)
        mult_dx(last)
        quant_dw(last)
        mult_dw(last)
        dx_out(1, 0, "s")
        dx_out(1, 1, "v")
        dx_turn(1, 0)
        dx_turn(1, 1)
        store_dw(last, "sv")
        dx_dst = out_0[1].rearrange("(p j) u -> p j u", j=J)
        dx_back(1, 0, "s")
        nc.scalar.dma_start(out=dx_dst[:, 0:2, :], in_=dx_parts[1][1][:, 0:2, :])
        dx_back(1, 1, "v")
        nc.sync.dma_start(out=dx_dst[:, 2:4, :], in_=dx_parts[1][1][:, 2:4, :])
